import numpy as np
import ml_dtypes


def mxq(x, axis, fmt="e4m3"):
    dtype, down = {"e4m3": (ml_dtypes.float8_e4m3fn, 7), "e5m2": (ml_dtypes.float8_e5m2, 14)}[fmt]
    v = np.moveaxis(np.asarray(x, np.float32).astype(ml_dtypes.bfloat16).astype(np.float64), axis, -1)
    blocks = v.reshape(v.shape[:-1] + (-1, 32))
    amax = np.abs(blocks).max(-1, keepdims=True)
    byte = np.maximum(np.where(amax > 0, np.frexp(amax)[1] - 1 + 127, 0) - down, 1)
    scale = np.exp2(byte - 127.0)
    codes = (blocks / scale).astype(np.float32).astype(dtype).astype(np.float64)
    return np.moveaxis((codes * scale).reshape(v.shape), -1, axis)


WIDE = False


def mx_kscale(k):
    if not WIDE:
        return np.ones(k)
    levels = np.array([10, -10, 5, -5, 0])
    a = np.random.permutation(np.resize(levels, k // 512 * 4)).reshape(k // 512, 4)
    idx = np.arange(k)
    return np.exp2(a[idx // 512, idx % 128 // 32])


BF16 = ml_dtypes.bfloat16


def bf(x):
    return np.asarray(x, np.float32).astype(BF16)


def f64(x):
    return np.asarray(x).astype(np.float64)


N, F, K, D, E = 512, 2048, 1536, 1024, 1024
SIG = 2.0
PS = 16.0


def setup_inputs():
    t, sx = mx_kscale(K), mx_kscale(F)
    s = np.concatenate([sx, np.ones(E)])
    g = SIG * np.random.standard_normal((N, K))
    e = np.exp(g - g.max(-1, keepdims=True))
    w = e / e.sum(-1, keepdims=True) * (np.random.uniform(size=K) * PS)[None, :]
    return {"att_prior": bf(w * t[None, :]),
            "dic": bf(np.random.standard_normal((K, D)) / t[:, None]),
            "x": bf(np.random.standard_normal((N, F)) * sx[None, :]),
            "cs_w": bf(np.random.standard_normal((K, F + E)) * (F + E) ** -0.5 / s[None, :]),
            "cs_b": bf(np.random.standard_normal(K) * 0.1)}


def reference(att_prior, dic, x, cs_w, cs_b):
    z = mxq(f64(att_prior), 1, "e4m3") @ mxq(f64(dic), 0, "e4m3")
    xz = np.concatenate([f64(x), z], axis=1)
    causal_logits = (mxq(xz, 1, "e4m3") @ mxq(f64(cs_w), 1, "e4m3").T) + f64(cs_b)
    return causal_logits, z

@@ -1,0 +1,246 @@
+from contextlib import ExitStack
+
+import concourse.mybir as mybir
+from concourse.masks import make_identity
+
+F32 = mybir.dt.float32
+BF16 = mybir.dt.bfloat16
+U32 = mybir.dt.uint32
+U8 = mybir.dt.uint8
+FP8X4 = mybir.dt.float8_e4m3fn_x4
+
+P = 128
+PACK = 4
+K_PASS = P * PACK
+ROWS = 512
+ROW_TILES = ROWS // P
+
+TOKENS, DICT, Z_DIM, X_DIM, OUT_DIM = 512, 1536, 1024, 2048, 1536
+XZ_DIM = X_DIM + Z_DIM
+DICT_PASSES = DICT // K_PASS
+X_PASSES = X_DIM // K_PASS
+Z_PASSES = Z_DIM // K_PASS
+XZ_PASSES = XZ_DIM // K_PASS
+
+RUN_PASSES = 2
+LOAD_K = RUN_PASSES * K_PASS
+RUNS_PER_CHUNK = XZ_PASSES // RUN_PASSES
+CHUNKS = OUT_DIM // ROWS
+W_RUNS = CHUNKS * RUNS_PER_CHUNK
+LEAD = 2
+
+FIRST_LOADS = 13
+FIRST_W_LOADS = FIRST_LOADS - 7
+
+FLOPS = 2 * TOKENS * DICT * Z_DIM + 2 * TOKENS * XZ_DIM * OUT_DIM
+
+
+def tile_visualdeconfounder_pb_kernel(tc, att_prior, dic, x, cs_w, cs_b, out_0, out_1):
+    nc = tc.nc
+    logits_out, z_out = out_0, out_1
+
+    with ExitStack() as ctx:
+        const = ctx.enter_context(tc.tile_pool(name="const", bufs=1))
+        keep = ctx.enter_context(tc.tile_pool(name="keep", bufs=1))
+        raw_pool = ctx.enter_context(tc.tile_pool(name="raw", bufs=FIRST_LOADS))
+        grouped_pool = ctx.enter_context(tc.tile_pool(name="grouped", bufs=6))
+        chunk_pool = ctx.enter_context(tc.tile_pool(name="chunk", bufs=2))
+        result_pool = ctx.enter_context(tc.tile_pool(name="result", bufs=4))
+        transposed = ctx.enter_context(tc.psum_pool(name="transposed", bufs=4))
+        sums = ctx.enter_context(tc.psum_pool(name="sums", bufs=4))
+        ctx.enter_context(tc.manual_schedule())
+
+        def load_k_last(matrix, row0, k0, width):
+            raw = raw_pool.tile([P, ROW_TILES, LOAD_K], BF16, tag="raw")
+            nc.sync.dma_start(
+                out=raw[:, :, 0:width],
+                in_=matrix[row0 : row0 + ROWS, k0 : k0 + width].rearrange("(t p) k -> p t k", p=P),
+            )
+            return raw
+
+        def load_dic(c):
+            raw = raw_pool.tile([P, PACK, Z_DIM], BF16, tag="raw")
+            nc.sync.dma_start(
+                out=raw[:].rearrange("p (u e) d -> p u e d", u=2),
+                in_=dic[c * K_PASS : (c + 1) * K_PASS, :].rearrange("(u p e) d -> p u e d", u=2, e=2),
+            )
+            return raw
+
+        def load_w(j):
+            chunk, r = divmod(j, RUNS_PER_CHUNK)
+            return load_k_last(cs_w, chunk * ROWS, r * LOAD_K, LOAD_K)
+
+        att_raw = [load_k_last(att_prior, 0, 0, LOAD_K), load_k_last(att_prior, 0, LOAD_K, DICT - LOAD_K)]
+        dic_raw = [load_dic(c) for c in range(DICT_PASSES)]
+        x_raw = [load_k_last(x, 0, r * LOAD_K, LOAD_K) for r in range(X_DIM // LOAD_K)]
+        w_raw = [load_w(j) for j in range(FIRST_W_LOADS)]
+        bias = const.tile([P, OUT_DIM], BF16)
+        nc.sync.dma_start(out=bias[:], in_=cs_b.partition_broadcast(P))
+
+        identity = const.tile([P, P], F32)
+        make_identity(nc, identity[:])
+
+        att_codes = keep.tile([P, DICT_PASSES, TOKENS], U32, align_bytes=64)
+        att_scales = keep.tile([P, DICT_PASSES, TOKENS], U8, align_bytes=64)
+        dic_codes = keep.tile([P, DICT_PASSES, Z_DIM], U32, align_bytes=64)
+        dic_scales = keep.tile([P, DICT_PASSES, Z_DIM], U8, align_bytes=64)
+        xz_codes = keep.tile([P, XZ_PASSES, TOKENS], U32, align_bytes=64)
+        xz_scales = keep.tile([P, XZ_PASSES, TOKENS], U8, align_bytes=64)
+        z_sb = keep.tile([P, ROW_TILES, Z_DIM], F32)
+
+        def empty_bank(bank_in_run, out, in_):
+            if bank_in_run % 4 == 3:
+                nc.vector.tensor_copy(out=out, in_=in_)
+            else:
+                nc.scalar.copy(out=out, in_=in_)
+
+        def transpose_run(raw, passes):
+            grouped_tiles = []
+            for s in range(passes):
+                grouped = grouped_pool.tile([P, PACK * ROWS], BF16, tag="grouped", align_bytes=64)
+                pairs = grouped[:].bitcast(F32).rearrange("p (r u) -> p r u", u=2)
+                for half in range(2):
+                    bank = transposed.tile([P, 2, 2 * P], F32, tag="bank")
+                    for u in range(2):
+                        for i in range(2):
+                            words = raw[:, 2 * half + i, :].bitcast(F32)
+                            first = (2 * s + u) * P
+                            nc.tensor.transpose(
+                                bank[:, u, i * P : (i + 1) * P], words[:, first : first + P], identity[:]
+                            )
+                    empty_bank(
+                        2 * s + half,
+                        pairs[:, half * 2 * P : (half + 1) * 2 * P, :],
+                        bank[:].rearrange("p u r -> p r u"),
+                    )
+                grouped_tiles.append(grouped)
+            return grouped_tiles
+
+        def quantise_run(grouped_tiles, codes, scales, first_pass):
+            for s, grouped in enumerate(grouped_tiles):
+                nc.vector.quantize_mx(
+                    out=codes[:, first_pass + s, :].bitcast(FP8X4),
+                    scales=scales[:, first_pass + s, :],
+                    in_=grouped[:],
+                )
+
+        att_grouped = transpose_run(att_raw[0], RUN_PASSES) + transpose_run(att_raw[1], 1)
+        quantise_run(att_grouped, att_codes, att_scales, 0)
+
+        def regroup_dic(piece):
+            c, h = divmod(piece, 2)
+            grouped = grouped_pool.tile([P, PACK * ROWS], BF16, tag="grouped", align_bytes=64)
+            dst = grouped[:].rearrange("p (c i t) -> p c t i", i=4, t=PACK)
+            src = dic_raw[c][:, :, h * ROWS : (h + 1) * ROWS].rearrange("p t (c i) -> p c t i", i=4)
+            middle = ROWS // 4 // 2
+            nc.vector.tensor_copy(out=dst[:, 0:middle], in_=src[:, 0:middle])
+            nc.scalar.copy(out=dst[:, middle:], in_=src[:, middle:])
+            return grouped
+
+        z_sums = {}
+        for h in range(2):
+            for t in range(ROW_TILES):
+                if h == 0:
+                    bank = transposed.tile([P, ROWS], F32, tag="bank")
+                else:
+                    bank = sums.tile([P, ROWS], F32, tag="sum")
+                z_sums[(t, h)] = bank
+
+        pieces = 2 * DICT_PASSES
+        dic_grouped = [regroup_dic(0)]
+        for piece in range(pieces):
+            c, h = divmod(piece, 2)
+            if piece + 1 < pieces:
+                dic_grouped.append(regroup_dic(piece + 1))
+            columns = slice(h * ROWS, (h + 1) * ROWS)
+            nc.vector.quantize_mx(
+                out=dic_codes[:, c, columns].bitcast(FP8X4),
+                scales=dic_scales[:, c, columns],
+                in_=dic_grouped[piece][:],
+            )
+            for t in range(ROW_TILES):
+                nc.tensor.matmul_mx(
+                    out=z_sums[(t, h)][:],
+                    lhsT=att_codes[:, c, t * P : (t + 1) * P].bitcast(FP8X4),
+                    lhsT_scale=att_scales[:, c, t * P : (t + 1) * P],
+                    rhs=dic_codes[:, c, columns].bitcast(FP8X4),
+                    rhs_scale=dic_scales[:, c, columns],
+                    start=(c == 0),
+                    stop=(c == DICT_PASSES - 1),
+                )
+
+        w_raw.extend([load_w(j) for j in range(FIRST_W_LOADS, W_RUNS)])
+
+        for h in range(2):
+            for t in range(ROW_TILES):
+                empty_bank(t, z_sb[:, t, h * ROWS : (h + 1) * ROWS], z_sums[(t, h)][:])
+        for t in range(ROW_TILES):
+            nc.sync.dma_start(out=z_out[t * P : (t + 1) * P, :], in_=z_sb[:, t, :])
+
+        def transpose_z(s):
+            grouped = grouped_pool.tile([P, PACK * TOKENS], BF16, tag="grouped", align_bytes=64)
+            by_token = grouped[:].rearrange("p (n t) -> p n t", t=PACK)
+            for t in range(ROW_TILES):
+                every_second = z_sb[:, t, :].rearrange("p (s u q e) -> p s u e q", s=Z_PASSES, u=2, e=2)
+                bank = transposed.tile([P, PACK, P], F32, tag="bank")
+                for u in range(2):
+                    for e in range(2):
+                        nc.tensor.transpose(bank[:, 2 * u + e, :], every_second[:, s, u, e, :], identity[:])
+                empty_bank(t, by_token[:, t * P : (t + 1) * P, :], bank[:].rearrange("p t n -> p n t"))
+            return [grouped]
+
+        w_codes, w_scales, logit_sums = [], [], []
+
+        def quantise_w(j, grouped_tiles):
+            chunk, r = divmod(j, RUNS_PER_CHUNK)
+            if r == 0:
+                codes = chunk_pool.tile([P, XZ_PASSES, ROWS], U32, tag="w_codes", align_bytes=64)
+                scales = chunk_pool.tile([P, XZ_PASSES, ROWS], U8, tag="w_scales", align_bytes=64)
+                w_codes.append(codes)
+                w_scales.append(scales)
+            quantise_run(grouped_tiles, w_codes[chunk], w_scales[chunk], r * RUN_PASSES)
+
+        def multiply_w(j):
+            chunk, r = divmod(j, RUNS_PER_CHUNK)
+            columns = slice(chunk * ROWS, (chunk + 1) * ROWS)
+            for t in range(ROW_TILES):
+                if r == 0:
+                    bank = sums.tile([P, ROWS], F32, tag="sum")
+                    logit_sums.append(bank)
+                bank = logit_sums[chunk * ROW_TILES + t]
+                for g in range(r * RUN_PASSES, (r + 1) * RUN_PASSES):
+                    nc.tensor.matmul_mx(
+                        out=bank[:],
+                        lhsT=xz_codes[:, g, t * P : (t + 1) * P].bitcast(FP8X4),
+                        lhsT_scale=xz_scales[:, g, t * P : (t + 1) * P],
+                        rhs=w_codes[chunk][:, g, :].bitcast(FP8X4),
+                        rhs_scale=w_scales[chunk][:, g, :],
+                        start=(g == 0),
+                        stop=(g == XZ_PASSES - 1),
+                    )
+                if r == RUNS_PER_CHUNK - 1:
+                    result = result_pool.tile([P, ROWS], F32, tag="result")
+                    nc.vector.tensor_tensor(
+                        out=result[:], in0=bank[:], in1=bias[:, columns], op=mybir.AluOpType.add
+                    )
+                    nc.sync.dma_start(out=logits_out[t * P : (t + 1) * P, columns], in_=result[:])
+
+        x_grouped_0 = transpose_run(x_raw[0], RUN_PASSES)
+        x_grouped_1 = transpose_run(x_raw[1], RUN_PASSES)
+        quantise_run(x_grouped_0, xz_codes, xz_scales, 0)
+        z_grouped_0 = transpose_z(0)
+        quantise_run(x_grouped_1, xz_codes, xz_scales, RUN_PASSES)
+        z_grouped_1 = transpose_z(1)
+        quantise_run(z_grouped_0, xz_codes, xz_scales, X_PASSES)
+        w_grouped = [transpose_run(w_raw[0], RUN_PASSES)]
+        quantise_run(z_grouped_1, xz_codes, xz_scales, X_PASSES + 1)
+        for j in range(1, LEAD):
+            w_grouped.append(transpose_run(w_raw[j], RUN_PASSES))
+            quantise_w(j - 1, w_grouped[j - 1])
+
+        for j in range(W_RUNS):
+            if j + LEAD < W_RUNS:
+                w_grouped.append(transpose_run(w_raw[j + LEAD], RUN_PASSES))
+            if j + LEAD - 1 < W_RUNS:
+                quantise_w(j + LEAD - 1, w_grouped[j + LEAD - 1])
+            multiply_w(j)

@@ -27,7 +27,8 @@ LOAD_K = RUN_PASSES * K_PASS
 RUNS_PER_CHUNK = XZ_PASSES // RUN_PASSES
 CHUNKS = OUT_DIM // ROWS
 W_RUNS = CHUNKS * RUNS_PER_CHUNK
-LEAD = 2
+X_RUNS = X_PASSES // RUN_PASSES
+AHEAD = 2
 
 FIRST_LOADS = 13
 FIRST_W_LOADS = FIRST_LOADS - 7
@@ -89,7 +90,7 @@ def tile_visualdeconfounder_pb_kernel(tc, att_prior, dic, x, cs_w, cs_b, out_0, 
         z_sb = keep.tile([P, ROW_TILES, Z_DIM], F32)
 
         def empty_bank(bank_in_run, out, in_):
-            if bank_in_run % 4 == 3:
+            if bank_in_run % 4 == 0:
                 nc.vector.tensor_copy(out=out, in_=in_)
             else:
                 nc.scalar.copy(out=out, in_=in_)
@@ -124,8 +125,8 @@ def tile_visualdeconfounder_pb_kernel(tc, att_prior, dic, x, cs_w, cs_b, out_0, 
                     in_=grouped[:],
                 )
 
-        att_grouped = transpose_run(att_raw[0], RUN_PASSES) + transpose_run(att_raw[1], 1)
-        quantise_run(att_grouped, att_codes, att_scales, 0)
+        quantise_run(transpose_run(att_raw[0], RUN_PASSES), att_codes, att_scales, 0)
+        quantise_run(transpose_run(att_raw[1], 1), att_codes, att_scales, RUN_PASSES)
 
         def regroup_dic(piece):
             c, h = divmod(piece, 2)
@@ -191,8 +192,9 @@ def tile_visualdeconfounder_pb_kernel(tc, att_prior, dic, x, cs_w, cs_b, out_0, 
 
         w_codes, w_scales, logit_sums = [], [], []
 
-        def quantise_w(j, grouped_tiles):
+        def prepare_w(j):
             chunk, r = divmod(j, RUNS_PER_CHUNK)
+            grouped_tiles = transpose_run(w_raw[j], RUN_PASSES)
             if r == 0:
                 codes = chunk_pool.tile([P, XZ_PASSES, ROWS], U32, tag="w_codes", align_bytes=64)
                 scales = chunk_pool.tile([P, XZ_PASSES, ROWS], U8, tag="w_scales", align_bytes=64)
@@ -225,22 +227,12 @@ def tile_visualdeconfounder_pb_kernel(tc, att_prior, dic, x, cs_w, cs_b, out_0, 
                     )
                     nc.sync.dma_start(out=logits_out[t * P : (t + 1) * P, columns], in_=result[:])
 
-        x_grouped_0 = transpose_run(x_raw[0], RUN_PASSES)
-        x_grouped_1 = transpose_run(x_raw[1], RUN_PASSES)
-        quantise_run(x_grouped_0, xz_codes, xz_scales, 0)
-        z_grouped_0 = transpose_z(0)
-        quantise_run(x_grouped_1, xz_codes, xz_scales, RUN_PASSES)
-        z_grouped_1 = transpose_z(1)
-        quantise_run(z_grouped_0, xz_codes, xz_scales, X_PASSES)
-        w_grouped = [transpose_run(w_raw[0], RUN_PASSES)]
-        quantise_run(z_grouped_1, xz_codes, xz_scales, X_PASSES + 1)
-        for j in range(1, LEAD):
-            w_grouped.append(transpose_run(w_raw[j], RUN_PASSES))
-            quantise_w(j - 1, w_grouped[j - 1])
-
+        for r in range(X_RUNS):
+            quantise_run(transpose_run(x_raw[r], RUN_PASSES), xz_codes, xz_scales, r * RUN_PASSES)
+            prepare_w(r)
         for j in range(W_RUNS):
-            if j + LEAD < W_RUNS:
-                w_grouped.append(transpose_run(w_raw[j + LEAD], RUN_PASSES))
-            if j + LEAD - 1 < W_RUNS:
-                quantise_w(j + LEAD - 1, w_grouped[j + LEAD - 1])
             multiply_w(j)
+            if j < Z_PASSES:
+                quantise_run(transpose_z(j), xz_codes, xz_scales, X_PASSES + j)
+            if j + AHEAD < W_RUNS:
+                prepare_w(j + AHEAD)

from contextlib import ExitStack

import concourse.mybir as mybir
from concourse.masks import make_identity

F32 = mybir.dt.float32
BF16 = mybir.dt.bfloat16
U32 = mybir.dt.uint32
U8 = mybir.dt.uint8
FP8X4 = mybir.dt.float8_e4m3fn_x4

P = 128
PACK = 4
K_PASS = P * PACK
ROWS = 512
ROW_TILES = ROWS // P

TOKENS, DICT, Z_DIM, X_DIM, OUT_DIM = 512, 1536, 1024, 2048, 1536
XZ_DIM = X_DIM + Z_DIM
DICT_PASSES = DICT // K_PASS
X_PASSES = X_DIM // K_PASS
Z_PASSES = Z_DIM // K_PASS
XZ_PASSES = XZ_DIM // K_PASS

RUN_PASSES = 2
LOAD_K = RUN_PASSES * K_PASS
RUNS_PER_CHUNK = XZ_PASSES // RUN_PASSES
CHUNKS = OUT_DIM // ROWS
W_RUNS = CHUNKS * RUNS_PER_CHUNK
X_RUNS = X_PASSES // RUN_PASSES
AHEAD = 2

FIRST_LOADS = 13
FIRST_W_LOADS = FIRST_LOADS - 7

FLOPS = 2 * TOKENS * DICT * Z_DIM + 2 * TOKENS * XZ_DIM * OUT_DIM


def tile_visualdeconfounder_pb_kernel(tc, att_prior, dic, x, cs_w, cs_b, out_0, out_1):
    nc = tc.nc
    logits_out, z_out = out_0, out_1

    with ExitStack() as ctx:
        const = ctx.enter_context(tc.tile_pool(name="const", bufs=1))
        keep = ctx.enter_context(tc.tile_pool(name="keep", bufs=1))
        raw_pool = ctx.enter_context(tc.tile_pool(name="raw", bufs=FIRST_LOADS))
        grouped_pool = ctx.enter_context(tc.tile_pool(name="grouped", bufs=6))
        chunk_pool = ctx.enter_context(tc.tile_pool(name="chunk", bufs=2))
        result_pool = ctx.enter_context(tc.tile_pool(name="result", bufs=4))
        transposed = ctx.enter_context(tc.psum_pool(name="transposed", bufs=4))
        sums = ctx.enter_context(tc.psum_pool(name="sums", bufs=4))
        ctx.enter_context(tc.manual_schedule())

        def load_k_last(matrix, row0, k0, width):
            raw = raw_pool.tile([P, ROW_TILES, LOAD_K], BF16, tag="raw")
            nc.sync.dma_start(
                out=raw[:, :, 0:width],
                in_=matrix[row0 : row0 + ROWS, k0 : k0 + width].rearrange("(t p) k -> p t k", p=P),
            )
            return raw

        def load_dic(c):
            raw = raw_pool.tile([P, PACK, Z_DIM], BF16, tag="raw")
            nc.sync.dma_start(
                out=raw[:].rearrange("p (u e) d -> p u e d", u=2),
                in_=dic[c * K_PASS : (c + 1) * K_PASS, :].rearrange("(u p e) d -> p u e d", u=2, e=2),
            )
            return raw

        def load_w(j):
            chunk, r = divmod(j, RUNS_PER_CHUNK)
            return load_k_last(cs_w, chunk * ROWS, r * LOAD_K, LOAD_K)

        att_raw = [load_k_last(att_prior, 0, 0, LOAD_K), load_k_last(att_prior, 0, LOAD_K, DICT - LOAD_K)]
        dic_raw = [load_dic(c) for c in range(DICT_PASSES)]
        x_raw = [load_k_last(x, 0, r * LOAD_K, LOAD_K) for r in range(X_DIM // LOAD_K)]
        w_raw = [load_w(j) for j in range(FIRST_W_LOADS)]
        bias = const.tile([P, OUT_DIM], BF16)
        nc.sync.dma_start(out=bias[:], in_=cs_b.partition_broadcast(P))

        identity = const.tile([P, P], F32)
        make_identity(nc, identity[:])

        att_codes = keep.tile([P, DICT_PASSES, TOKENS], U32, align_bytes=64)
        att_scales = keep.tile([P, DICT_PASSES, TOKENS], U8, align_bytes=64)
        dic_codes = keep.tile([P, DICT_PASSES, Z_DIM], U32, align_bytes=64)
        dic_scales = keep.tile([P, DICT_PASSES, Z_DIM], U8, align_bytes=64)
        xz_codes = keep.tile([P, XZ_PASSES, TOKENS], U32, align_bytes=64)
        xz_scales = keep.tile([P, XZ_PASSES, TOKENS], U8, align_bytes=64)
        z_sb = keep.tile([P, ROW_TILES, Z_DIM], F32)

        def empty_bank(bank_in_run, out, in_):
            if bank_in_run % 4 == 0:
                nc.vector.tensor_copy(out=out, in_=in_)
            else:
                nc.scalar.copy(out=out, in_=in_)

        def transpose_run(raw, passes):
            grouped_tiles = []
            for s in range(passes):
                grouped = grouped_pool.tile([P, PACK * ROWS], BF16, tag="grouped", align_bytes=64)
                pairs = grouped[:].bitcast(F32).rearrange("p (r u) -> p r u", u=2)
                for half in range(2):
                    bank = transposed.tile([P, 2, 2 * P], F32, tag="bank")
                    for u in range(2):
                        for i in range(2):
                            words = raw[:, 2 * half + i, :].bitcast(F32)
                            first = (2 * s + u) * P
                            nc.tensor.transpose(
                                bank[:, u, i * P : (i + 1) * P], words[:, first : first + P], identity[:]
                            )
                    empty_bank(
                        2 * s + half,
                        pairs[:, half * 2 * P : (half + 1) * 2 * P, :],
                        bank[:].rearrange("p u r -> p r u"),
                    )
                grouped_tiles.append(grouped)
            return grouped_tiles

        def quantise_run(grouped_tiles, codes, scales, first_pass):
            for s, grouped in enumerate(grouped_tiles):
                nc.vector.quantize_mx(
                    out=codes[:, first_pass + s, :].bitcast(FP8X4),
                    scales=scales[:, first_pass + s, :],
                    in_=grouped[:],
                )

        quantise_run(transpose_run(att_raw[0], RUN_PASSES), att_codes, att_scales, 0)
        quantise_run(transpose_run(att_raw[1], 1), att_codes, att_scales, RUN_PASSES)

        def regroup_dic(piece):
            c, h = divmod(piece, 2)
            grouped = grouped_pool.tile([P, PACK * ROWS], BF16, tag="grouped", align_bytes=64)
            dst = grouped[:].rearrange("p (c i t) -> p c t i", i=4, t=PACK)
            src = dic_raw[c][:, :, h * ROWS : (h + 1) * ROWS].rearrange("p t (c i) -> p c t i", i=4)
            middle = ROWS // 4 // 2
            nc.vector.tensor_copy(out=dst[:, 0:middle], in_=src[:, 0:middle])
            nc.scalar.copy(out=dst[:, middle:], in_=src[:, middle:])
            return grouped

        z_sums = {}
        for h in range(2):
            for t in range(ROW_TILES):
                if h == 0:
                    bank = transposed.tile([P, ROWS], F32, tag="bank")
                else:
                    bank = sums.tile([P, ROWS], F32, tag="sum")
                z_sums[(t, h)] = bank

        pieces = 2 * DICT_PASSES
        dic_grouped = [regroup_dic(0)]
        for piece in range(pieces):
            c, h = divmod(piece, 2)
            if piece + 1 < pieces:
                dic_grouped.append(regroup_dic(piece + 1))
            columns = slice(h * ROWS, (h + 1) * ROWS)
            nc.vector.quantize_mx(
                out=dic_codes[:, c, columns].bitcast(FP8X4),
                scales=dic_scales[:, c, columns],
                in_=dic_grouped[piece][:],
            )
            for t in range(ROW_TILES):
                nc.tensor.matmul_mx(
                    out=z_sums[(t, h)][:],
                    lhsT=att_codes[:, c, t * P : (t + 1) * P].bitcast(FP8X4),
                    lhsT_scale=att_scales[:, c, t * P : (t + 1) * P],
                    rhs=dic_codes[:, c, columns].bitcast(FP8X4),
                    rhs_scale=dic_scales[:, c, columns],
                    start=(c == 0),
                    stop=(c == DICT_PASSES - 1),
                )

        w_raw.extend([load_w(j) for j in range(FIRST_W_LOADS, W_RUNS)])

        for h in range(2):
            for t in range(ROW_TILES):
                empty_bank(t, z_sb[:, t, h * ROWS : (h + 1) * ROWS], z_sums[(t, h)][:])
        for t in range(ROW_TILES):
            nc.sync.dma_start(out=z_out[t * P : (t + 1) * P, :], in_=z_sb[:, t, :])

        def transpose_z(s):
            grouped = grouped_pool.tile([P, PACK * TOKENS], BF16, tag="grouped", align_bytes=64)
            by_token = grouped[:].rearrange("p (n t) -> p n t", t=PACK)
            for t in range(ROW_TILES):
                every_second = z_sb[:, t, :].rearrange("p (s u q e) -> p s u e q", s=Z_PASSES, u=2, e=2)
                bank = transposed.tile([P, PACK, P], F32, tag="bank")
                for u in range(2):
                    for e in range(2):
                        nc.tensor.transpose(bank[:, 2 * u + e, :], every_second[:, s, u, e, :], identity[:])
                empty_bank(t, by_token[:, t * P : (t + 1) * P, :], bank[:].rearrange("p t n -> p n t"))
            return [grouped]

        w_codes, w_scales, logit_sums = [], [], []

        def prepare_w(j):
            chunk, r = divmod(j, RUNS_PER_CHUNK)
            grouped_tiles = transpose_run(w_raw[j], RUN_PASSES)
            if r == 0:
                codes = chunk_pool.tile([P, XZ_PASSES, ROWS], U32, tag="w_codes", align_bytes=64)
                scales = chunk_pool.tile([P, XZ_PASSES, ROWS], U8, tag="w_scales", align_bytes=64)
                w_codes.append(codes)
                w_scales.append(scales)
            quantise_run(grouped_tiles, w_codes[chunk], w_scales[chunk], r * RUN_PASSES)

        def multiply_w(j):
            chunk, r = divmod(j, RUNS_PER_CHUNK)
            columns = slice(chunk * ROWS, (chunk + 1) * ROWS)
            for t in range(ROW_TILES):
                if r == 0:
                    bank = sums.tile([P, ROWS], F32, tag="sum")
                    logit_sums.append(bank)
                bank = logit_sums[chunk * ROW_TILES + t]
                for g in range(r * RUN_PASSES, (r + 1) * RUN_PASSES):
                    nc.tensor.matmul_mx(
                        out=bank[:],
                        lhsT=xz_codes[:, g, t * P : (t + 1) * P].bitcast(FP8X4),
                        lhsT_scale=xz_scales[:, g, t * P : (t + 1) * P],
                        rhs=w_codes[chunk][:, g, :].bitcast(FP8X4),
                        rhs_scale=w_scales[chunk][:, g, :],
                        start=(g == 0),
                        stop=(g == XZ_PASSES - 1),
                    )
                if r == RUNS_PER_CHUNK - 1:
                    result = result_pool.tile([P, ROWS], F32, tag="result")
                    nc.vector.tensor_tensor(
                        out=result[:], in0=bank[:], in1=bias[:, columns], op=mybir.AluOpType.add
                    )
                    nc.sync.dma_start(out=logits_out[t * P : (t + 1) * P, columns], in_=result[:])

        for r in range(X_RUNS):
            quantise_run(transpose_run(x_raw[r], RUN_PASSES), xz_codes, xz_scales, r * RUN_PASSES)
            prepare_w(r)
        for j in range(W_RUNS):
            multiply_w(j)
            if j < Z_PASSES:
                quantise_run(transpose_z(j), xz_codes, xz_scales, X_PASSES + j)
            if j + AHEAD < W_RUNS:
                prepare_w(j + AHEAD)
